import numpy as np
import ml_dtypes


def mxq(x, axis, fmt="e4m3"):
    dtype, down = {"e4m3": (ml_dtypes.float8_e4m3fn, 7), "e5m2": (ml_dtypes.float8_e5m2, 14)}[fmt]
    v = np.moveaxis(np.asarray(x, np.float32).astype(ml_dtypes.bfloat16).astype(np.float64), axis, -1)
    blocks = v.reshape(v.shape[:-1] + (-1, 32))
    amax = np.abs(blocks).max(-1, keepdims=True)
    byte = np.maximum(np.where(amax > 0, np.frexp(amax)[1] - 1 + 127, 0) - down, 1)
    scale = np.exp2(byte - 127.0)
    codes = (blocks / scale).astype(np.float32).astype(dtype).astype(np.float64)
    return np.moveaxis((codes * scale).reshape(v.shape), -1, axis)


WIDE = False


def mx_kscale(k):
    if not WIDE:
        return np.ones(k)
    levels = np.array([10, -10, 5, -5, 0])
    a = np.random.permutation(np.resize(levels, k // 512 * 4)).reshape(k // 512, 4)
    idx = np.arange(k)
    return np.exp2(a[idx // 512, idx % 128 // 32])


BF16 = ml_dtypes.bfloat16


def bf(x):
    return np.asarray(x, np.float32).astype(BF16)


def f64(x):
    return np.asarray(x).astype(np.float64)


B, S, D, H, QK, EXP, V, FI, LI, T = 1, 1024, 1024, 2, 256, 2048, 1024, 512, 768, 512
W = 2 * QK + 2 * EXP


def erf(a):
    c = np.clip(a, -6.0, 6.0)
    term = c.copy()
    tot = c.copy()
    for n in range(1, 120):
        term = term * (2.0 * c * c / (2 * n + 1))
        tot = tot + term
    r = 2.0 / np.sqrt(np.pi) * np.exp(-c * c) * tot
    return np.where(np.abs(a) > 6.0, np.sign(a), r)


def gelu(v):
    return 0.5 * v * (1.0 + erf(v / np.sqrt(2.0)))


def setup_inputs():
    s = mx_kscale(D)
    rows = np.concatenate([np.full(2 * QK, 1.5), np.ones(2 * EXP)])[:, None] / np.sqrt(D)
    x = np.random.standard_normal((B, S, D)) * (0.5 + np.random.random((B, S, 1))) + 0.3 * np.random.standard_normal((B, S, 1))
    return {"x": bf(x),
            "norm_w": bf((1.0 + 0.1 * np.random.standard_normal(D)) * s),
            "expand_w": bf(np.random.standard_normal((W, D)) * rows / s[None, :])}


def reference(x, norm_w, expand_w):
    x = f64(x)
    mu = x.mean(-1, keepdims=True)
    xc = x - mu
    var = (xc * xc).mean(-1, keepdims=True)
    xn = xc / np.sqrt(var + 1e-5) * f64(norm_w)
    proj = mxq(xn, 2, "e4m3") @ mxq(f64(expand_w), 1, "e4m3").T
    q = proj[..., :QK]
    k = proj[..., QK:2 * QK]
    lin = proj[..., 2 * QK:2 * QK + EXP]
    pre = proj[..., 2 * QK + EXP:]
    geglu = lin * gelu(pre)
    return q, k, geglu

@@ -1,0 +1,248 @@
+from contextlib import ExitStack
+
+import concourse.mybir as mybir
+from concourse.masks import make_identity
+
+F32 = mybir.dt.float32
+BF16 = mybir.dt.bfloat16
+U32 = mybir.dt.uint32
+U8 = mybir.dt.uint8
+FP8X4 = mybir.dt.float8_e4m3fn_x4
+ALU = mybir.AluOpType
+ACT = mybir.ActivationFunctionType
+
+P = 128
+PACK = 4
+K = 1024
+K_PASS = P * PACK
+PASSES = K // K_PASS
+TOKENS = 1024
+TOKEN_TILES = TOKENS // P
+QK = 256
+EXP = 2048
+CHUNK = 512
+ROW_TILES = CHUNK // P
+PAIRS = EXP // CHUNK
+CHUNKS = 2 * PAIRS + 1
+QK_CHUNK = CHUNKS - 1
+SWEEP_TILES = 4
+STEP_TILES = 2
+AHEAD = 2
+EPS = 1e-5
+BN_MAX = 512
+
+FLOPS = 2 * TOKENS * K * (2 * QK + 2 * EXP)
+
+
+def chunk_first_row(c):
+    if c == QK_CHUNK:
+        return 0
+    return 2 * QK + (c % 2) * EXP + (c // 2) * CHUNK
+
+
+def tile_latentattentionblock_pa_kernel(tc, x, norm_w, expand_w, out_0, out_1, out_2):
+    nc = tc.nc
+    x_rows = x.flatten_outer_dims().rearrange("(p m) k -> p m k", m=TOKEN_TILES)
+    q_rows = out_0.flatten_outer_dims().rearrange("(p m) n -> p m n", m=TOKEN_TILES)
+    k_rows = out_1.flatten_outer_dims().rearrange("(p m) n -> p m n", m=TOKEN_TILES)
+    geglu_rows = out_2.flatten_outer_dims().rearrange("(p m) n -> p m n", m=TOKEN_TILES)
+
+    with ExitStack() as stack:
+        keep = stack.enter_context(tc.tile_pool(name="keep", bufs=1))
+        small = stack.enter_context(tc.tile_pool(name="small", bufs=3))
+        work = stack.enter_context(tc.tile_pool(name="work", bufs=2))
+        results = stack.enter_context(tc.tile_pool(name="results", bufs=3))
+        banks = stack.enter_context(tc.psum_pool(name="banks", bufs=8))
+        stack.enter_context(tc.manual_schedule())
+
+        x_in = [keep.tile([P, STEP_TILES, K], BF16, name="x_in%d" % i) for i in range(TOKEN_TILES // STEP_TILES)]
+        w_in = [keep.tile([P, ROW_TILES, K], BF16, name="w_in%d" % c) for c in range(CHUNKS)]
+
+        def load_tokens(i):
+            nc.sync.dma_start(out=x_in[i][:], in_=x_rows[:, STEP_TILES * i : STEP_TILES * (i + 1), :])
+
+        def load_weights(c):
+            first = chunk_first_row(c)
+            nc.sync.dma_start(
+                out=w_in[c][:],
+                in_=expand_w[first : first + CHUNK, :].rearrange("(i p) k -> p i k", p=P),
+            )
+
+        gain = keep.tile([P, 2 * PASSES, 2], BF16, name="gain")
+        with nc.allow_non_contiguous_dma(reason="1,024 gains, two to a piece, once"):
+            nc.scalar.dma_start(out=gain[:], in_=norm_w.rearrange("(a p e) -> p a e", p=P, e=2))
+        gain_cols = gain[:].rearrange("p a e -> p (a e)")
+
+        for i in range(SWEEP_TILES // STEP_TILES):
+            load_tokens(i)
+        for c in range(CHUNKS):
+            load_weights(c)
+            if c % 2 == 0 and 0 < c // 2 < len(x_in) - 1:
+                load_tokens(c // 2 + 1)
+
+        ident = keep.tile([P, P], F32, name="ident")
+        make_identity(nc, ident[:])
+        minus_half = keep.tile([P, 1], F32, name="minus_half")
+        nc.gpsimd.memset(minus_half[:], -0.5)
+        warm = keep.tile([P, 1], F32, name="warm")
+        nc.scalar.activation(out=warm[:], in_=minus_half[:], func=ACT.Gelu)
+
+        x_codes = [keep.tile([P, PASSES * P], U32, name="x_codes%d" % m, align_bytes=64) for m in range(TOKEN_TILES)]
+        x_scales = [keep.tile([P, PASSES * P], U8, name="x_scales%d" % m, align_bytes=64) for m in range(TOKEN_TILES)]
+        w_codes = [keep.tile([P, PASSES * CHUNK], U32, name="w_codes%d" % c, align_bytes=64) for c in range(CHUNKS)]
+        w_scales = [keep.tile([P, PASSES * CHUNK], U8, name="w_scales%d" % c, align_bytes=64) for c in range(CHUNKS)]
+        normed = {}
+        x_grouped = {}
+        w_grouped = {}
+
+        def normalise(m):
+            xm = x_in[m // STEP_TILES][:, m % STEP_TILES, :]
+            stats = small.tile([P, K // BN_MAX, 6], F32, name="stats")
+            for h in range(K // BN_MAX):
+                nc.vector.bn_stats(out=stats[:, h, :], in_=xm[:, BN_MAX * h : BN_MAX * (h + 1)])
+            mean_var = small.tile([P, 2], F32, name="mean_var")
+            nc.vector.bn_aggr(out=mean_var[:], in_=stats[:].rearrange("p h s -> p (h s)"))
+            neg_mean = small.tile([P, 1], F32, name="neg_mean")
+            nc.gpsimd.tensor_scalar(
+                out=neg_mean[:], in0=mean_var[:, 0:1], scalar1=-1.0, scalar2=0.0, op0=ALU.mult, op1=ALU.add
+            )
+            var_eps = small.tile([P, 1], F32, name="var_eps")
+            nc.gpsimd.tensor_scalar(
+                out=var_eps[:], in0=mean_var[:, 1:2], scalar1=1.0, scalar2=EPS, op0=ALU.mult, op1=ALU.add
+            )
+            rstd = small.tile([P, 1], F32, name="rstd")
+            nc.gpsimd.tensor_tensor(out=rstd[:], in0=var_eps[:], in1=minus_half[:], op=ALU.pow)
+            y = work.tile([P, K], F32, name="y", bufs=SWEEP_TILES)
+            nc.gpsimd.tensor_scalar(
+                out=y[:].rearrange("r (a e q) -> r a e q", e=2, q=P),
+                in0=xm.rearrange("r (a q e) -> r a e q", e=2, q=P),
+                scalar1=neg_mean[:],
+                scalar2=rstd[:],
+                op0=ALU.add,
+                op1=ALU.mult,
+            )
+            normed[m] = y
+
+        def transpose_tokens(m):
+            y = normed[m]
+            grouped = work.tile([P, PASSES, P, PACK], BF16, name="x_grouped", align_bytes=64)
+            for g in range(PASSES):
+                yt = banks.tile([P, PACK, P], F32, name="yt", tag="bank")
+                for t in range(PACK):
+                    block = PACK * g + t
+                    nc.tensor.transpose(yt[:, t, :], y[:, P * block : P * (block + 1)], ident[:])
+                nc.vector.tensor_tensor(
+                    out=grouped[:, g, :, :],
+                    in0=yt[:].rearrange("p t r -> p r t"),
+                    in1=gain_cols[:, PACK * g : PACK * (g + 1)].unsqueeze(1).to_broadcast([P, P, PACK]),
+                    op=ALU.mult,
+                )
+            x_grouped[m] = grouped
+
+        def quantise_tokens(m):
+            nc.vector.quantize_mx(
+                out=x_codes[m][:].bitcast(FP8X4),
+                scales=x_scales[m][:],
+                in_=x_grouped[m][:].rearrange("p g r t -> p (g r t)"),
+            )
+
+        def transpose_weights(c):
+            words = w_in[c][:].bitcast(F32)
+            grouped = work.tile([P, PASSES, CHUNK, PACK], BF16, name="w_grouped", bufs=3, align_bytes=64)
+            grouped_words = grouped[:].bitcast(F32)
+            for i in range(ROW_TILES):
+                wt = banks.tile([P, 2 * PASSES, P], F32, name="wt", tag="bank")
+                for a in range(2 * PASSES):
+                    nc.tensor.transpose(wt[:, a, :], words[:, i, P * a : P * (a + 1)], ident[:])
+                nc.scalar.copy(
+                    out=grouped_words[:, :, P * i : P * (i + 1), :],
+                    in_=wt[:].rearrange("p (g u) n -> p g n u", u=2),
+                )
+            w_grouped[c] = grouped
+
+        def quantise_weights(c):
+            nc.vector.quantize_mx(
+                out=w_codes[c][:].bitcast(FP8X4),
+                scales=w_scales[c][:],
+                in_=w_grouped[c][:].rearrange("p g n t -> p (g n t)"),
+            )
+
+        def project(m, c):
+            acc = banks.tile([P, CHUNK], F32, name="acc", tag="bank")
+            for g in range(PASSES):
+                nc.tensor.matmul_mx(
+                    out=acc[:],
+                    lhsT=x_codes[m][:, P * g : P * (g + 1)].bitcast(FP8X4),
+                    lhsT_scale=x_scales[m][:, P * g : P * (g + 1)],
+                    rhs=w_codes[c][:, CHUNK * g : CHUNK * (g + 1)].bitcast(FP8X4),
+                    rhs_scale=w_scales[c][:, CHUNK * g : CHUNK * (g + 1)],
+                    start=(g == 0),
+                    stop=(g == PASSES - 1),
+                )
+            return acc
+
+        def gated_step(pair, first_tile):
+            gated = results.tile([P, STEP_TILES, CHUNK], F32, name="gated")
+            for i in range(STEP_TILES):
+                lin = project(first_tile + i, 2 * pair)
+                pre = project(first_tile + i, 2 * pair + 1)
+                gate = results.tile([P, CHUNK], F32, name="gate")
+                nc.scalar.activation(out=gate[:], in_=pre[:], func=ACT.Gelu)
+                nc.vector.tensor_tensor(out=gated[:, i, :], in0=lin[:], in1=gate[:], op=ALU.mult)
+            nc.sync.dma_start(
+                out=geglu_rows[:, first_tile : first_tile + STEP_TILES, CHUNK * pair : CHUNK * (pair + 1)],
+                in_=gated[:],
+            )
+
+        def qk_step(first_tile):
+            for h in range(SWEEP_TILES // STEP_TILES):
+                first = first_tile + STEP_TILES * h
+                qk = results.tile([P, STEP_TILES, CHUNK], F32, name="qk", tag="gated")
+                for i in range(STEP_TILES):
+                    acc = project(first + i, QK_CHUNK)
+                    if i % 2 == 0:
+                        nc.scalar.copy(out=qk[:, i, :], in_=acc[:])
+                    else:
+                        nc.vector.tensor_copy(out=qk[:, i, :], in_=acc[:])
+                nc.sync.dma_start(out=q_rows[:, first : first + STEP_TILES, :], in_=qk[:, :, 0:QK])
+                nc.sync.dma_start(out=k_rows[:, first : first + STEP_TILES, :], in_=qk[:, :, QK : 2 * QK])
+
+        def step(first_tile, s):
+            if s < 2 * PAIRS:
+                gated_step(s // 2, first_tile + STEP_TILES * (s % 2))
+            else:
+                qk_step(first_tile)
+
+        for m in range(SWEEP_TILES):
+            normalise(m)
+        transpose_tokens(0)
+        transpose_weights(0)
+        transpose_tokens(1)
+        transpose_weights(1)
+        quantise_tokens(0)
+        quantise_tokens(1)
+        quantise_weights(0)
+        transpose_tokens(2)
+        transpose_weights(2)
+        quantise_weights(1)
+        transpose_tokens(3)
+        quantise_tokens(2)
+        quantise_tokens(3)
+
+        for s in range(CHUNKS):
+            step(0, s)
+            if s + AHEAD < CHUNKS:
+                quantise_weights(s + AHEAD)
+            if s + AHEAD + 1 < CHUNKS:
+                transpose_weights(s + AHEAD + 1)
+            late = SWEEP_TILES + (s - 1) // 2
+            if s % 2 == 1:
+                if s > 1:
+                    quantise_tokens(late - 1)
+                normalise(late)
+            elif s > 0:
+                transpose_tokens(late)
+        quantise_tokens(TOKEN_TILES - 1)
+
+        for s in range(CHUNKS):
+            step(SWEEP_TILES, s)

@@ -102,24 +102,23 @@ def tile_latentattentionblock_pa_kernel(tc, x, norm_w, expand_w, out_0, out_1, o
                 nc.vector.bn_stats(out=stats[:, h, :], in_=xm[:, BN_MAX * h : BN_MAX * (h + 1)])
             mean_var = small.tile([P, 2], F32, name="mean_var")
             nc.vector.bn_aggr(out=mean_var[:], in_=stats[:].rearrange("p h s -> p (h s)"))
-            neg_mean = small.tile([P, 1], F32, name="neg_mean")
-            nc.gpsimd.tensor_scalar(
-                out=neg_mean[:], in0=mean_var[:, 0:1], scalar1=-1.0, scalar2=0.0, op0=ALU.mult, op1=ALU.add
-            )
             var_eps = small.tile([P, 1], F32, name="var_eps")
             nc.gpsimd.tensor_scalar(
                 out=var_eps[:], in0=mean_var[:, 1:2], scalar1=1.0, scalar2=EPS, op0=ALU.mult, op1=ALU.add
             )
             rstd = small.tile([P, 1], F32, name="rstd")
             nc.gpsimd.tensor_tensor(out=rstd[:], in0=var_eps[:], in1=minus_half[:], op=ALU.pow)
-            y = work.tile([P, K], F32, name="y", bufs=SWEEP_TILES)
+            shift = small.tile([P, 1], F32, name="shift")
             nc.gpsimd.tensor_scalar(
+                out=shift[:], in0=mean_var[:, 0:1], scalar1=rstd[:], scalar2=-1.0, op0=ALU.mult, op1=ALU.mult
+            )
+            y = work.tile([P, K], F32, name="y")
+            nc.scalar.activation(
                 out=y[:].rearrange("r (a e q) -> r a e q", e=2, q=P),
-                in0=xm.rearrange("r (a q e) -> r a e q", e=2, q=P),
-                scalar1=neg_mean[:],
-                scalar2=rstd[:],
-                op0=ALU.add,
-                op1=ALU.mult,
+                in_=xm.rearrange("r (a q e) -> r a e q", e=2, q=P),
+                func=ACT.Identity,
+                bias=shift[:],
+                scale=rstd[:],
             )
             normed[m] = y
 
@@ -213,12 +212,14 @@ def tile_latentattentionblock_pa_kernel(tc, x, norm_w, expand_w, out_0, out_1, o
             else:
                 qk_step(first_tile)
 
-        for m in range(SWEEP_TILES):
-            normalise(m)
+        normalise(0)
+        normalise(1)
         transpose_tokens(0)
         transpose_weights(0)
+        normalise(2)
         transpose_tokens(1)
         transpose_weights(1)
+        normalise(3)
         quantise_tokens(0)
         quantise_tokens(1)
         quantise_weights(0)

@@ -27,7 +27,7 @@ CHUNKS = 2 * PAIRS + 1
 QK_CHUNK = CHUNKS - 1
 SWEEP_TILES = 4
 STEP_TILES = 2
-AHEAD = 2
+AHEAD = 3
 EPS = 1e-5
 BN_MAX = 512
 
@@ -102,23 +102,24 @@ def tile_latentattentionblock_pa_kernel(tc, x, norm_w, expand_w, out_0, out_1, o
                 nc.vector.bn_stats(out=stats[:, h, :], in_=xm[:, BN_MAX * h : BN_MAX * (h + 1)])
             mean_var = small.tile([P, 2], F32, name="mean_var")
             nc.vector.bn_aggr(out=mean_var[:], in_=stats[:].rearrange("p h s -> p (h s)"))
+            neg_mean = small.tile([P, 1], F32, name="neg_mean")
+            nc.gpsimd.tensor_scalar(
+                out=neg_mean[:], in0=mean_var[:, 0:1], scalar1=-1.0, scalar2=0.0, op0=ALU.mult, op1=ALU.add
+            )
             var_eps = small.tile([P, 1], F32, name="var_eps")
             nc.gpsimd.tensor_scalar(
                 out=var_eps[:], in0=mean_var[:, 1:2], scalar1=1.0, scalar2=EPS, op0=ALU.mult, op1=ALU.add
             )
             rstd = small.tile([P, 1], F32, name="rstd")
             nc.gpsimd.tensor_tensor(out=rstd[:], in0=var_eps[:], in1=minus_half[:], op=ALU.pow)
-            shift = small.tile([P, 1], F32, name="shift")
+            y = work.tile([P, K], F32, name="y", bufs=SWEEP_TILES)
             nc.gpsimd.tensor_scalar(
-                out=shift[:], in0=mean_var[:, 0:1], scalar1=rstd[:], scalar2=-1.0, op0=ALU.mult, op1=ALU.mult
-            )
-            y = work.tile([P, K], F32, name="y")
-            nc.scalar.activation(
                 out=y[:].rearrange("r (a e q) -> r a e q", e=2, q=P),
-                in_=xm.rearrange("r (a q e) -> r a e q", e=2, q=P),
-                func=ACT.Identity,
-                bias=shift[:],
-                scale=rstd[:],
+                in0=xm.rearrange("r (a q e) -> r a e q", e=2, q=P),
+                scalar1=neg_mean[:],
+                scalar2=rstd[:],
+                op0=ALU.add,
+                op1=ALU.mult,
             )
             normed[m] = y
 
@@ -181,11 +182,11 @@ def tile_latentattentionblock_pa_kernel(tc, x, norm_w, expand_w, out_0, out_1, o
             return acc
 
         def gated_step(pair, first_tile):
-            gated = results.tile([P, STEP_TILES, CHUNK], F32, name="gated")
+            gated = results.tile([P, STEP_TILES, CHUNK], F32, name="gated", bufs=6)
             for i in range(STEP_TILES):
                 lin = project(first_tile + i, 2 * pair)
                 pre = project(first_tile + i, 2 * pair + 1)
-                gate = results.tile([P, CHUNK], F32, name="gate")
+                gate = results.tile([P, CHUNK], F32, name="gate", bufs=4)
                 nc.scalar.activation(out=gate[:], in_=pre[:], func=ACT.Gelu)
                 nc.vector.tensor_tensor(out=gated[:, i, :], in0=lin[:], in1=gate[:], op=ALU.mult)
             nc.sync.dma_start(
@@ -196,7 +197,7 @@ def tile_latentattentionblock_pa_kernel(tc, x, norm_w, expand_w, out_0, out_1, o
         def qk_step(first_tile):
             for h in range(SWEEP_TILES // STEP_TILES):
                 first = first_tile + STEP_TILES * h
-                qk = results.tile([P, STEP_TILES, CHUNK], F32, name="qk", tag="gated")
+                qk = results.tile([P, STEP_TILES, CHUNK], F32, name="qk", tag="gated", bufs=6)
                 for i in range(STEP_TILES):
                     acc = project(first + i, QK_CHUNK)
                     if i % 2 == 0:
@@ -212,14 +213,12 @@ def tile_latentattentionblock_pa_kernel(tc, x, norm_w, expand_w, out_0, out_1, o
             else:
                 qk_step(first_tile)
 
-        normalise(0)
-        normalise(1)
+        for m in range(SWEEP_TILES):
+            normalise(m)
         transpose_tokens(0)
         transpose_weights(0)
-        normalise(2)
         transpose_tokens(1)
         transpose_weights(1)
-        normalise(3)
         quantise_tokens(0)
         quantise_tokens(1)
         quantise_weights(0)
@@ -229,6 +228,8 @@ def tile_latentattentionblock_pa_kernel(tc, x, norm_w, expand_w, out_0, out_1, o
         transpose_tokens(3)
         quantise_tokens(2)
         quantise_tokens(3)
+        transpose_weights(3)
+        quantise_weights(2)
 
         for s in range(CHUNKS):
             step(0, s)
@@ -236,13 +237,12 @@ def tile_latentattentionblock_pa_kernel(tc, x, norm_w, expand_w, out_0, out_1, o
                 quantise_weights(s + AHEAD)
             if s + AHEAD + 1 < CHUNKS:
                 transpose_weights(s + AHEAD + 1)
-            late = SWEEP_TILES + (s - 1) // 2
-            if s % 2 == 1:
-                if s > 1:
-                    quantise_tokens(late - 1)
-                normalise(late)
-            elif s > 0:
-                transpose_tokens(late)
+            if s % 2 == 1 and s > 1:
+                quantise_tokens(SWEEP_TILES + (s - 3) // 2)
+            if s % 2 == 0 and s < 2 * SWEEP_TILES:
+                normalise(SWEEP_TILES + s // 2)
+            if s % 2 == 0 and s > 0:
+                transpose_tokens(SWEEP_TILES + (s - 2) // 2)
         quantise_tokens(TOKEN_TILES - 1)
 
         for s in range(CHUNKS):

@@ -28,6 +28,10 @@ QK_CHUNK = CHUNKS - 1
 SWEEP_TILES = 4
 STEP_TILES = 2
 AHEAD = 3
+QK_STEP = -1
+LATE_EVERY = 2
+LATE_TRANSPOSE = 3
+LATE_QUANTISE = 4
 EPS = 1e-5
 BN_MAX = 512
 
@@ -207,11 +211,21 @@ def tile_latentattentionblock_pa_kernel(tc, x, norm_w, expand_w, out_0, out_1, o
                 nc.sync.dma_start(out=q_rows[:, first : first + STEP_TILES, :], in_=qk[:, :, 0:QK])
                 nc.sync.dma_start(out=k_rows[:, first : first + STEP_TILES, :], in_=qk[:, :, QK : 2 * QK])
 
-        def step(first_tile, s):
-            if s < 2 * PAIRS:
-                gated_step(s // 2, first_tile + STEP_TILES * (s % 2))
-            else:
-                qk_step(first_tile)
+        steps = []
+        for pair in range(PAIRS):
+            for half in range(SWEEP_TILES // STEP_TILES):
+                steps.append((pair, STEP_TILES * half))
+        steps.append((QK_STEP, 0))
+        for half in range(SWEEP_TILES // STEP_TILES):
+            for pair in range(PAIRS):
+                steps.append((pair, SWEEP_TILES + STEP_TILES * half))
+        steps.append((QK_STEP, SWEEP_TILES))
+
+        def late_tile(s, delay):
+            i, rest = divmod(s - delay, LATE_EVERY)
+            if rest == 0 and 0 <= i < TOKEN_TILES - SWEEP_TILES:
+                return SWEEP_TILES + i
+            return None
 
         for m in range(SWEEP_TILES):
             normalise(m)
@@ -231,19 +245,18 @@ def tile_latentattentionblock_pa_kernel(tc, x, norm_w, expand_w, out_0, out_1, o
         transpose_weights(3)
         quantise_weights(2)
 
-        for s in range(CHUNKS):
-            step(0, s)
+        for s, (pair, first_tile) in enumerate(steps):
+            if pair == QK_STEP:
+                qk_step(first_tile)
+            else:
+                gated_step(pair, first_tile)
             if s + AHEAD < CHUNKS:
                 quantise_weights(s + AHEAD)
             if s + AHEAD + 1 < CHUNKS:
                 transpose_weights(s + AHEAD + 1)
-            if s % 2 == 1 and s > 1:
-                quantise_tokens(SWEEP_TILES + (s - 3) // 2)
-            if s % 2 == 0 and s < 2 * SWEEP_TILES:
-                normalise(SWEEP_TILES + s // 2)
-            if s % 2 == 0 and s > 0:
-                transpose_tokens(SWEEP_TILES + (s - 2) // 2)
-        quantise_tokens(TOKEN_TILES - 1)
-
-        for s in range(CHUNKS):
-            step(SWEEP_TILES, s)
+            if late_tile(s, LATE_QUANTISE) is not None:
+                quantise_tokens(late_tile(s, LATE_QUANTISE))
+            if late_tile(s, 0) is not None:
+                normalise(late_tile(s, 0))
+            if late_tile(s, LATE_TRANSPOSE) is not None:
+                transpose_tokens(late_tile(s, LATE_TRANSPOSE))

@@ -16,6 +16,7 @@ PACK = 4
 K = 1024
 K_PASS = P * PACK
 PASSES = K // K_PASS
+QUARTERS = K // (2 * P)
 TOKENS = 1024
 TOKEN_TILES = TOKENS // P
 QK = 256
@@ -25,17 +26,26 @@ ROW_TILES = CHUNK // P
 PAIRS = EXP // CHUNK
 CHUNKS = 2 * PAIRS + 1
 QK_CHUNK = CHUNKS - 1
-SWEEP_TILES = 4
-STEP_TILES = 2
-AHEAD = 3
-QK_STEP = -1
-LATE_EVERY = 2
-LATE_TRANSPOSE = 3
-LATE_QUANTISE = 4
+PSUM_BANKS = 8
 EPS = 1e-5
 BN_MAX = 512
 
+SWEEP_TILES = 4
+STEP_TILES = 2
+QK_STEP = -1
+AHEAD = 3
+LATE_EVERY = 2
+LATE_TRANSPOSE = 3
+LATE_QUANTISE = 4
+
+W_GROUPED_BUFS = 3
+X_GROUPED_BUFS = 2
+GATE_BUFS = 2 * STEP_TILES
+OUT_BUFS = 6 * STEP_TILES
+
 FLOPS = 2 * TOKENS * K * (2 * QK + 2 * EXP)
+
+assert SWEEP_TILES == AHEAD + 1
 
 
 def chunk_first_row(c):
@@ -46,24 +56,24 @@ def chunk_first_row(c):
 
 def tile_latentattentionblock_pa_kernel(tc, x, norm_w, expand_w, out_0, out_1, out_2):
     nc = tc.nc
-    x_rows = x.flatten_outer_dims().rearrange("(p m) k -> p m k", m=TOKEN_TILES)
-    q_rows = out_0.flatten_outer_dims().rearrange("(p m) n -> p m n", m=TOKEN_TILES)
-    k_rows = out_1.flatten_outer_dims().rearrange("(p m) n -> p m n", m=TOKEN_TILES)
-    geglu_rows = out_2.flatten_outer_dims().rearrange("(p m) n -> p m n", m=TOKEN_TILES)
+    x_rows = x.flatten_outer_dims().rearrange("(m p) k -> p m k", p=P)
+    q_rows = out_0.flatten_outer_dims().rearrange("(m p) n -> p m n", p=P)
+    k_rows = out_1.flatten_outer_dims().rearrange("(m p) n -> p m n", p=P)
+    geglu_rows = out_2.flatten_outer_dims().rearrange("(m p) n -> p m n", p=P)
 
     with ExitStack() as stack:
         keep = stack.enter_context(tc.tile_pool(name="keep", bufs=1))
-        small = stack.enter_context(tc.tile_pool(name="small", bufs=3))
-        work = stack.enter_context(tc.tile_pool(name="work", bufs=2))
-        results = stack.enter_context(tc.tile_pool(name="results", bufs=3))
-        banks = stack.enter_context(tc.psum_pool(name="banks", bufs=8))
+        small = stack.enter_context(tc.tile_pool(name="small", bufs=SWEEP_TILES))
+        work = stack.enter_context(tc.tile_pool(name="work", bufs=SWEEP_TILES))
+        results = stack.enter_context(tc.tile_pool(name="results", bufs=OUT_BUFS))
+        banks = stack.enter_context(tc.psum_pool(name="banks", bufs=PSUM_BANKS))
         stack.enter_context(tc.manual_schedule())
 
-        x_in = [keep.tile([P, STEP_TILES, K], BF16, name="x_in%d" % i) for i in range(TOKEN_TILES // STEP_TILES)]
+        x_in = [keep.tile([P, K], BF16, name="x_in%d" % m) for m in range(TOKEN_TILES)]
         w_in = [keep.tile([P, ROW_TILES, K], BF16, name="w_in%d" % c) for c in range(CHUNKS)]
 
-        def load_tokens(i):
-            nc.sync.dma_start(out=x_in[i][:], in_=x_rows[:, STEP_TILES * i : STEP_TILES * (i + 1), :])
+        def load_tokens(m):
+            nc.sync.dma_start(out=x_in[m][:], in_=x_rows[:, m, :])
 
         def load_weights(c):
             first = chunk_first_row(c)
@@ -72,17 +82,18 @@ def tile_latentattentionblock_pa_kernel(tc, x, norm_w, expand_w, out_0, out_1, o
                 in_=expand_w[first : first + CHUNK, :].rearrange("(i p) k -> p i k", p=P),
             )
 
-        gain = keep.tile([P, 2 * PASSES, 2], BF16, name="gain")
+        gain = keep.tile([P, QUARTERS, 2], BF16, name="gain")
         with nc.allow_non_contiguous_dma(reason="1,024 gains, two to a piece, once"):
             nc.scalar.dma_start(out=gain[:], in_=norm_w.rearrange("(a p e) -> p a e", p=P, e=2))
         gain_cols = gain[:].rearrange("p a e -> p (a e)")
 
-        for i in range(SWEEP_TILES // STEP_TILES):
-            load_tokens(i)
+        for m in range(SWEEP_TILES):
+            load_tokens(m)
         for c in range(CHUNKS):
             load_weights(c)
-            if c % 2 == 0 and 0 < c // 2 < len(x_in) - 1:
-                load_tokens(c // 2 + 1)
+            if c % 2 == 0 and SWEEP_TILES <= c + 2 < TOKEN_TILES:
+                load_tokens(c + 2)
+                load_tokens(c + 3)
 
         ident = keep.tile([P, P], F32, name="ident")
         make_identity(nc, ident[:])
@@ -100,7 +111,7 @@ def tile_latentattentionblock_pa_kernel(tc, x, norm_w, expand_w, out_0, out_1, o
         w_grouped = {}
 
         def normalise(m):
-            xm = x_in[m // STEP_TILES][:, m % STEP_TILES, :]
+            xm = x_in[m][:]
             stats = small.tile([P, K // BN_MAX, 6], F32, name="stats")
             for h in range(K // BN_MAX):
                 nc.vector.bn_stats(out=stats[:, h, :], in_=xm[:, BN_MAX * h : BN_MAX * (h + 1)])
@@ -116,7 +127,7 @@ def tile_latentattentionblock_pa_kernel(tc, x, norm_w, expand_w, out_0, out_1, o
             )
             rstd = small.tile([P, 1], F32, name="rstd")
             nc.gpsimd.tensor_tensor(out=rstd[:], in0=var_eps[:], in1=minus_half[:], op=ALU.pow)
-            y = work.tile([P, K], F32, name="y", bufs=SWEEP_TILES)
+            y = work.tile([P, K], F32, name="y")
             nc.gpsimd.tensor_scalar(
                 out=y[:].rearrange("r (a e q) -> r a e q", e=2, q=P),
                 in0=xm.rearrange("r (a q e) -> r a e q", e=2, q=P),
@@ -129,7 +140,7 @@ def tile_latentattentionblock_pa_kernel(tc, x, norm_w, expand_w, out_0, out_1, o
 
         def transpose_tokens(m):
             y = normed[m]
-            grouped = work.tile([P, PASSES, P, PACK], BF16, name="x_grouped", align_bytes=64)
+            grouped = work.tile([P, PASSES, P, PACK], BF16, name="x_grouped", bufs=X_GROUPED_BUFS, align_bytes=64)
             for g in range(PASSES):
                 yt = banks.tile([P, PACK, P], F32, name="yt", tag="bank")
                 for t in range(PACK):
@@ -152,11 +163,11 @@ def tile_latentattentionblock_pa_kernel(tc, x, norm_w, expand_w, out_0, out_1, o
 
         def transpose_weights(c):
             words = w_in[c][:].bitcast(F32)
-            grouped = work.tile([P, PASSES, CHUNK, PACK], BF16, name="w_grouped", bufs=3, align_bytes=64)
+            grouped = work.tile([P, PASSES, CHUNK, PACK], BF16, name="w_grouped", bufs=W_GROUPED_BUFS, align_bytes=64)
             grouped_words = grouped[:].bitcast(F32)
             for i in range(ROW_TILES):
-                wt = banks.tile([P, 2 * PASSES, P], F32, name="wt", tag="bank")
-                for a in range(2 * PASSES):
+                wt = banks.tile([P, QUARTERS, P], F32, name="wt", tag="bank")
+                for a in range(QUARTERS):
                     nc.tensor.transpose(wt[:, a, :], words[:, i, P * a : P * (a + 1)], ident[:])
                 nc.scalar.copy(
                     out=grouped_words[:, :, P * i : P * (i + 1), :],
@@ -186,30 +197,25 @@ def tile_latentattentionblock_pa_kernel(tc, x, norm_w, expand_w, out_0, out_1, o
             return acc
 
         def gated_step(pair, first_tile):
-            gated = results.tile([P, STEP_TILES, CHUNK], F32, name="gated", bufs=6)
-            for i in range(STEP_TILES):
-                lin = project(first_tile + i, 2 * pair)
-                pre = project(first_tile + i, 2 * pair + 1)
-                gate = results.tile([P, CHUNK], F32, name="gate", bufs=4)
+            for m in range(first_tile, first_tile + STEP_TILES):
+                lin = project(m, 2 * pair)
+                pre = project(m, 2 * pair + 1)
+                gate = results.tile([P, CHUNK], F32, name="gate", bufs=GATE_BUFS)
                 nc.scalar.activation(out=gate[:], in_=pre[:], func=ACT.Gelu)
-                nc.vector.tensor_tensor(out=gated[:, i, :], in0=lin[:], in1=gate[:], op=ALU.mult)
-            nc.sync.dma_start(
-                out=geglu_rows[:, first_tile : first_tile + STEP_TILES, CHUNK * pair : CHUNK * (pair + 1)],
-                in_=gated[:],
-            )
+                gated = results.tile([P, CHUNK], F32, name="gated", tag="out")
+                nc.vector.tensor_tensor(out=gated[:], in0=lin[:], in1=gate[:], op=ALU.mult)
+                nc.sync.dma_start(out=geglu_rows[:, m, CHUNK * pair : CHUNK * (pair + 1)], in_=gated[:])
 
         def qk_step(first_tile):
-            for h in range(SWEEP_TILES // STEP_TILES):
-                first = first_tile + STEP_TILES * h
-                qk = results.tile([P, STEP_TILES, CHUNK], F32, name="qk", tag="gated", bufs=6)
-                for i in range(STEP_TILES):
-                    acc = project(first + i, QK_CHUNK)
-                    if i % 2 == 0:
-                        nc.scalar.copy(out=qk[:, i, :], in_=acc[:])
-                    else:
-                        nc.vector.tensor_copy(out=qk[:, i, :], in_=acc[:])
-                nc.sync.dma_start(out=q_rows[:, first : first + STEP_TILES, :], in_=qk[:, :, 0:QK])
-                nc.sync.dma_start(out=k_rows[:, first : first + STEP_TILES, :], in_=qk[:, :, QK : 2 * QK])
+            for m in range(first_tile, first_tile + SWEEP_TILES):
+                acc = project(m, QK_CHUNK)
+                qk = results.tile([P, CHUNK], F32, name="qk", tag="out")
+                if m % 2 == 0:
+                    nc.scalar.copy(out=qk[:], in_=acc[:])
+                else:
+                    nc.vector.tensor_copy(out=qk[:], in_=acc[:])
+                nc.sync.dma_start(out=q_rows[:, m, :], in_=qk[:, 0:QK])
+                nc.sync.dma_start(out=k_rows[:, m, :], in_=qk[:, QK : 2 * QK])
 
         steps = []
         for pair in range(PAIRS):
@@ -229,21 +235,14 @@ def tile_latentattentionblock_pa_kernel(tc, x, norm_w, expand_w, out_0, out_1, o
 
         for m in range(SWEEP_TILES):
             normalise(m)
-        transpose_tokens(0)
-        transpose_weights(0)
-        transpose_tokens(1)
-        transpose_weights(1)
-        quantise_tokens(0)
-        quantise_tokens(1)
-        quantise_weights(0)
-        transpose_tokens(2)
-        transpose_weights(2)
-        quantise_weights(1)
-        transpose_tokens(3)
-        quantise_tokens(2)
-        quantise_tokens(3)
-        transpose_weights(3)
-        quantise_weights(2)
+        for m in range(SWEEP_TILES):
+            transpose_tokens(m)
+            transpose_weights(m)
+            if m % STEP_TILES == STEP_TILES - 1:
+                for ready in range(m - STEP_TILES + 1, m + 1):
+                    quantise_tokens(ready)
+            if m > 0:
+                quantise_weights(m - 1)
 
         for s, (pair, first_tile) in enumerate(steps):
             if pair == QK_STEP:

@@ -87,9 +87,12 @@ def tile_latentattentionblock_pa_kernel(tc, x, norm_w, expand_w, out_0, out_1, o
             nc.scalar.dma_start(out=gain[:], in_=norm_w.rearrange("(a p e) -> p a e", p=P, e=2))
         gain_cols = gain[:].rearrange("p a e -> p (a e)")
 
-        for m in range(SWEEP_TILES):
+        for m in range(STEP_TILES):
             load_tokens(m)
-        for c in range(CHUNKS):
+        load_weights(0)
+        for m in range(STEP_TILES, SWEEP_TILES):
+            load_tokens(m)
+        for c in range(1, CHUNKS):
             load_weights(c)
             if c % 2 == 0 and SWEEP_TILES <= c + 2 < TOKEN_TILES:
                 load_tokens(c + 2)
@@ -236,8 +239,8 @@ def tile_latentattentionblock_pa_kernel(tc, x, norm_w, expand_w, out_0, out_1, o
         for m in range(SWEEP_TILES):
             normalise(m)
         for m in range(SWEEP_TILES):
-            transpose_tokens(m)
             transpose_weights(m)
+            transpose_tokens(m)
             if m % STEP_TILES == STEP_TILES - 1:
                 for ready in range(m - STEP_TILES + 1, m + 1):
                     quantise_tokens(ready)

@@ -94,16 +94,16 @@ def tile_latentattentionblock_pa_kernel(tc, x, norm_w, expand_w, out_0, out_1, o
             load_tokens(m)
         for c in range(1, CHUNKS):
             load_weights(c)
-            if c % 2 == 0 and SWEEP_TILES <= c + 2 < TOKEN_TILES:
+            if c % 2 == 1 and SWEEP_TILES <= c + 1 < TOKEN_TILES:
+                load_tokens(c + 1)
                 load_tokens(c + 2)
-                load_tokens(c + 3)
 
         ident = keep.tile([P, P], F32, name="ident")
         make_identity(nc, ident[:])
-        minus_half = keep.tile([P, 1], F32, name="minus_half")
+        minus_half = keep.tile([P, STEP_TILES], F32, name="minus_half")
         nc.gpsimd.memset(minus_half[:], -0.5)
         warm = keep.tile([P, 1], F32, name="warm")
-        nc.scalar.activation(out=warm[:], in_=minus_half[:], func=ACT.Gelu)
+        nc.scalar.activation(out=warm[:], in_=minus_half[:, 0:1], func=ACT.Gelu)
 
         x_codes = [keep.tile([P, PASSES * P], U32, name="x_codes%d" % m, align_bytes=64) for m in range(TOKEN_TILES)]
         x_scales = [keep.tile([P, PASSES * P], U8, name="x_scales%d" % m, align_bytes=64) for m in range(TOKEN_TILES)]
@@ -113,33 +113,35 @@ def tile_latentattentionblock_pa_kernel(tc, x, norm_w, expand_w, out_0, out_1, o
         x_grouped = {}
         w_grouped = {}
 
-        def normalise(m):
-            xm = x_in[m][:]
-            stats = small.tile([P, K // BN_MAX, 6], F32, name="stats")
-            for h in range(K // BN_MAX):
-                nc.vector.bn_stats(out=stats[:, h, :], in_=xm[:, BN_MAX * h : BN_MAX * (h + 1)])
-            mean_var = small.tile([P, 2], F32, name="mean_var")
-            nc.vector.bn_aggr(out=mean_var[:], in_=stats[:].rearrange("p h s -> p (h s)"))
-            neg_mean = small.tile([P, 1], F32, name="neg_mean")
+        def normalise(tiles):
+            count = len(tiles)
+            mean_var = small.tile([P, count, 2], F32, name="mean_var")
+            for i, m in enumerate(tiles):
+                stats = small.tile([P, K // BN_MAX, 6], F32, name="stats")
+                for h in range(K // BN_MAX):
+                    nc.vector.bn_stats(out=stats[:, h, :], in_=x_in[m][:, BN_MAX * h : BN_MAX * (h + 1)])
+                nc.vector.bn_aggr(out=mean_var[:, i, :], in_=stats[:].rearrange("p h s -> p (h s)"))
+            neg_mean = small.tile([P, count], F32, name="neg_mean")
             nc.gpsimd.tensor_scalar(
-                out=neg_mean[:], in0=mean_var[:, 0:1], scalar1=-1.0, scalar2=0.0, op0=ALU.mult, op1=ALU.add
+                out=neg_mean[:], in0=mean_var[:, :, 0], scalar1=-1.0, scalar2=0.0, op0=ALU.mult, op1=ALU.add
             )
-            var_eps = small.tile([P, 1], F32, name="var_eps")
+            var_eps = small.tile([P, count], F32, name="var_eps")
             nc.gpsimd.tensor_scalar(
-                out=var_eps[:], in0=mean_var[:, 1:2], scalar1=1.0, scalar2=EPS, op0=ALU.mult, op1=ALU.add
+                out=var_eps[:], in0=mean_var[:, :, 1], scalar1=1.0, scalar2=EPS, op0=ALU.mult, op1=ALU.add
             )
-            rstd = small.tile([P, 1], F32, name="rstd")
-            nc.gpsimd.tensor_tensor(out=rstd[:], in0=var_eps[:], in1=minus_half[:], op=ALU.pow)
-            y = work.tile([P, K], F32, name="y")
-            nc.gpsimd.tensor_scalar(
-                out=y[:].rearrange("r (a e q) -> r a e q", e=2, q=P),
-                in0=xm.rearrange("r (a q e) -> r a e q", e=2, q=P),
-                scalar1=neg_mean[:],
-                scalar2=rstd[:],
-                op0=ALU.add,
-                op1=ALU.mult,
-            )
-            normed[m] = y
+            rstd = small.tile([P, count], F32, name="rstd")
+            nc.gpsimd.tensor_tensor(out=rstd[:], in0=var_eps[:], in1=minus_half[:, 0:count], op=ALU.pow)
+            for i, m in enumerate(tiles):
+                y = work.tile([P, K], F32, name="y")
+                nc.gpsimd.tensor_scalar(
+                    out=y[:].rearrange("r (a e q) -> r a e q", e=2, q=P),
+                    in0=x_in[m][:].rearrange("r (a q e) -> r a e q", e=2, q=P),
+                    scalar1=neg_mean[:, i : i + 1],
+                    scalar2=rstd[:, i : i + 1],
+                    op0=ALU.add,
+                    op1=ALU.mult,
+                )
+                normed[m] = y
 
         def transpose_tokens(m):
             y = normed[m]
@@ -236,16 +238,18 @@ def tile_latentattentionblock_pa_kernel(tc, x, norm_w, expand_w, out_0, out_1, o
                 return SWEEP_TILES + i
             return None
 
-        for m in range(SWEEP_TILES):
-            normalise(m)
+        for m in range(STEP_TILES):
+            normalise([m])
+        normalise(list(range(STEP_TILES, SWEEP_TILES)))
         for m in range(SWEEP_TILES):
             transpose_weights(m)
+            if 0 < m < SWEEP_TILES - 1:
+                quantise_weights(m - 1)
             transpose_tokens(m)
             if m % STEP_TILES == STEP_TILES - 1:
                 for ready in range(m - STEP_TILES + 1, m + 1):
                     quantise_tokens(ready)
-            if m > 0:
-                quantise_weights(m - 1)
+        quantise_weights(SWEEP_TILES - 2)
 
         for s, (pair, first_tile) in enumerate(steps):
             if pair == QK_STEP:
@@ -259,6 +263,6 @@ def tile_latentattentionblock_pa_kernel(tc, x, norm_w, expand_w, out_0, out_1, o
             if late_tile(s, LATE_QUANTISE) is not None:
                 quantise_tokens(late_tile(s, LATE_QUANTISE))
             if late_tile(s, 0) is not None:
-                normalise(late_tile(s, 0))
+                normalise([late_tile(s, 0)])
             if late_tile(s, LATE_TRANSPOSE) is not None:
                 transpose_tokens(late_tile(s, LATE_TRANSPOSE))

@@ -51,7 +51,7 @@ assert SWEEP_TILES == AHEAD + 1
 def chunk_first_row(c):
     if c == QK_CHUNK:
         return 0
-    return 2 * QK + (c % 2) * EXP + (c // 2) * CHUNK
+    return 2 * QK + (1 - c % 2) * EXP + (c // 2) * CHUNK
 
 
 def tile_latentattentionblock_pa_kernel(tc, x, norm_w, expand_w, out_0, out_1, out_2):
@@ -203,8 +203,8 @@ def tile_latentattentionblock_pa_kernel(tc, x, norm_w, expand_w, out_0, out_1, o
 
         def gated_step(pair, first_tile):
             for m in range(first_tile, first_tile + STEP_TILES):
-                lin = project(m, 2 * pair)
-                pre = project(m, 2 * pair + 1)
+                pre = project(m, 2 * pair)
+                lin = project(m, 2 * pair + 1)
                 gate = results.tile([P, CHUNK], F32, name="gate", bufs=GATE_BUFS)
                 nc.scalar.activation(out=gate[:], in_=pre[:], func=ACT.Gelu)
                 gated = results.tile([P, CHUNK], F32, name="gated", tag="out")

@@ -38,6 +38,8 @@ LATE_EVERY = 2
 LATE_TRANSPOSE = 3
 LATE_QUANTISE = 4
 
+END_PIECES = 2
+
 W_GROUPED_BUFS = 3
 X_GROUPED_BUFS = 2
 GATE_BUFS = 2 * STEP_TILES
@@ -73,7 +75,9 @@ def tile_latentattentionblock_pa_kernel(tc, x, norm_w, expand_w, out_0, out_1, o
         w_in = [keep.tile([P, ROW_TILES, K], BF16, name="w_in%d" % c) for c in range(CHUNKS)]
 
         def load_tokens(m):
-            nc.sync.dma_start(out=x_in[m][:], in_=x_rows[:, m, :])
+            pieces = K // BN_MAX if m == 0 else 1
+            for columns in [slice(K // pieces * h, K // pieces * (h + 1)) for h in range(pieces)]:
+                nc.sync.dma_start(out=x_in[m][:, columns], in_=x_rows[:, m, columns])
 
         def load_weights(c):
             first = chunk_first_row(c)
@@ -187,29 +191,37 @@ def tile_latentattentionblock_pa_kernel(tc, x, norm_w, expand_w, out_0, out_1, o
                 in_=w_grouped[c][:].rearrange("p g n t -> p (g n t)"),
             )
 
-        def project(m, c):
-            acc = banks.tile([P, CHUNK], F32, name="acc", tag="bank")
+        def project(m, c, first=0, width=CHUNK):
+            acc = banks.tile([P, width], F32, name="acc", tag="bank")
             for g in range(PASSES):
+                features = slice(CHUNK * g + first, CHUNK * g + first + width)
                 nc.tensor.matmul_mx(
                     out=acc[:],
                     lhsT=x_codes[m][:, P * g : P * (g + 1)].bitcast(FP8X4),
                     lhsT_scale=x_scales[m][:, P * g : P * (g + 1)],
-                    rhs=w_codes[c][:, CHUNK * g : CHUNK * (g + 1)].bitcast(FP8X4),
-                    rhs_scale=w_scales[c][:, CHUNK * g : CHUNK * (g + 1)],
+                    rhs=w_codes[c][:, features].bitcast(FP8X4),
+                    rhs_scale=w_scales[c][:, features],
                     start=(g == 0),
                     stop=(g == PASSES - 1),
                 )
             return acc
 
-        def gated_step(pair, first_tile):
-            for m in range(first_tile, first_tile + STEP_TILES):
+        def gated_step(pair, first_tile, last_pieces=1):
+            tiles = range(first_tile, first_tile + STEP_TILES)
+            gates = {}
+            for m in tiles:
                 pre = project(m, 2 * pair)
-                lin = project(m, 2 * pair + 1)
-                gate = results.tile([P, CHUNK], F32, name="gate", bufs=GATE_BUFS)
-                nc.scalar.activation(out=gate[:], in_=pre[:], func=ACT.Gelu)
-                gated = results.tile([P, CHUNK], F32, name="gated", tag="out")
-                nc.vector.tensor_tensor(out=gated[:], in0=lin[:], in1=gate[:], op=ALU.mult)
-                nc.sync.dma_start(out=geglu_rows[:, m, CHUNK * pair : CHUNK * (pair + 1)], in_=gated[:])
+                gates[m] = results.tile([P, CHUNK], F32, name="gate", bufs=GATE_BUFS)
+                nc.scalar.activation(out=gates[m][:], in_=pre[:], func=ACT.Gelu)
+            for m in tiles:
+                width = CHUNK // (last_pieces if m == tiles[-1] else 1)
+                for first in range(0, CHUNK, width):
+                    lin = project(m, 2 * pair + 1, first, width)
+                    gated = results.tile([P, width], F32, name="gated", tag="out")
+                    nc.vector.tensor_tensor(out=gated[:], in0=lin[:], in1=gates[m][:, first : first + width], op=ALU.mult)
+                    nc.sync.dma_start(
+                        out=geglu_rows[:, m, CHUNK * pair + first : CHUNK * pair + first + width], in_=gated[:]
+                    )
 
         def qk_step(first_tile):
             for m in range(first_tile, first_tile + SWEEP_TILES):
@@ -228,9 +240,10 @@ def tile_latentattentionblock_pa_kernel(tc, x, norm_w, expand_w, out_0, out_1, o
                 steps.append((pair, STEP_TILES * half))
         steps.append((QK_STEP, 0))
         for half in range(SWEEP_TILES // STEP_TILES):
+            if half == SWEEP_TILES // STEP_TILES - 1:
+                steps.append((QK_STEP, SWEEP_TILES))
             for pair in range(PAIRS):
                 steps.append((pair, SWEEP_TILES + STEP_TILES * half))
-        steps.append((QK_STEP, SWEEP_TILES))
 
         def late_tile(s, delay):
             i, rest = divmod(s - delay, LATE_EVERY)
@@ -255,7 +268,7 @@ def tile_latentattentionblock_pa_kernel(tc, x, norm_w, expand_w, out_0, out_1, o
             if pair == QK_STEP:
                 qk_step(first_tile)
             else:
-                gated_step(pair, first_tile)
+                gated_step(pair, first_tile, last_pieces=(END_PIECES if s == len(steps) - 1 else 1))
             if s + AHEAD < CHUNKS:
                 quantise_weights(s + AHEAD)
             if s + AHEAD + 1 < CHUNKS:

@@ -87,12 +87,13 @@ def tile_latentattentionblock_pa_kernel(tc, x, norm_w, expand_w, out_0, out_1, o
             )
 
         gain = keep.tile([P, QUARTERS, 2], BF16, name="gain")
-        with nc.allow_non_contiguous_dma(reason="1,024 gains, two to a piece, once"):
-            nc.scalar.dma_start(out=gain[:], in_=norm_w.rearrange("(a p e) -> p a e", p=P, e=2))
         gain_cols = gain[:].rearrange("p a e -> p (a e)")
 
         for m in range(STEP_TILES):
             load_tokens(m)
+            if m == 0:
+                with nc.allow_non_contiguous_dma(reason="1,024 gains, two to a piece, once"):
+                    nc.sync.dma_start(out=gain[:], in_=norm_w.rearrange("(a p e) -> p a e", p=P, e=2))
         load_weights(0)
         for m in range(STEP_TILES, SWEEP_TILES):
             load_tokens(m)

from contextlib import ExitStack

import concourse.mybir as mybir
from concourse.masks import make_identity

F32 = mybir.dt.float32
BF16 = mybir.dt.bfloat16
U32 = mybir.dt.uint32
U8 = mybir.dt.uint8
FP8X4 = mybir.dt.float8_e4m3fn_x4
ALU = mybir.AluOpType
ACT = mybir.ActivationFunctionType

P = 128
PACK = 4
K = 1024
K_PASS = P * PACK
PASSES = K // K_PASS
QUARTERS = K // (2 * P)
TOKENS = 1024
TOKEN_TILES = TOKENS // P
QK = 256
EXP = 2048
CHUNK = 512
ROW_TILES = CHUNK // P
PAIRS = EXP // CHUNK
CHUNKS = 2 * PAIRS + 1
QK_CHUNK = CHUNKS - 1
PSUM_BANKS = 8
EPS = 1e-5
BN_MAX = 512

SWEEP_TILES = 4
STEP_TILES = 2
QK_STEP = -1
AHEAD = 3
LATE_EVERY = 2
LATE_TRANSPOSE = 3
LATE_QUANTISE = 4

END_PIECES = 2

W_GROUPED_BUFS = 3
X_GROUPED_BUFS = 2
GATE_BUFS = 2 * STEP_TILES
OUT_BUFS = 6 * STEP_TILES

FLOPS = 2 * TOKENS * K * (2 * QK + 2 * EXP)

assert SWEEP_TILES == AHEAD + 1


def chunk_first_row(c):
    if c == QK_CHUNK:
        return 0
    return 2 * QK + (1 - c % 2) * EXP + (c // 2) * CHUNK


def tile_latentattentionblock_pa_kernel(tc, x, norm_w, expand_w, out_0, out_1, out_2):
    nc = tc.nc
    x_rows = x.flatten_outer_dims().rearrange("(m p) k -> p m k", p=P)
    q_rows = out_0.flatten_outer_dims().rearrange("(m p) n -> p m n", p=P)
    k_rows = out_1.flatten_outer_dims().rearrange("(m p) n -> p m n", p=P)
    geglu_rows = out_2.flatten_outer_dims().rearrange("(m p) n -> p m n", p=P)

    with ExitStack() as stack:
        keep = stack.enter_context(tc.tile_pool(name="keep", bufs=1))
        small = stack.enter_context(tc.tile_pool(name="small", bufs=SWEEP_TILES))
        work = stack.enter_context(tc.tile_pool(name="work", bufs=SWEEP_TILES))
        results = stack.enter_context(tc.tile_pool(name="results", bufs=OUT_BUFS))
        banks = stack.enter_context(tc.psum_pool(name="banks", bufs=PSUM_BANKS))
        stack.enter_context(tc.manual_schedule())

        x_in = [keep.tile([P, K], BF16, name="x_in%d" % m) for m in range(TOKEN_TILES)]
        w_in = [keep.tile([P, ROW_TILES, K], BF16, name="w_in%d" % c) for c in range(CHUNKS)]

        def load_tokens(m):
            pieces = K // BN_MAX if m == 0 else 1
            for columns in [slice(K // pieces * h, K // pieces * (h + 1)) for h in range(pieces)]:
                nc.sync.dma_start(out=x_in[m][:, columns], in_=x_rows[:, m, columns])

        def load_weights(c):
            first = chunk_first_row(c)
            nc.sync.dma_start(
                out=w_in[c][:],
                in_=expand_w[first : first + CHUNK, :].rearrange("(i p) k -> p i k", p=P),
            )

        gain = keep.tile([P, QUARTERS, 2], BF16, name="gain")
        gain_cols = gain[:].rearrange("p a e -> p (a e)")

        for m in range(STEP_TILES):
            load_tokens(m)
            if m == 0:
                with nc.allow_non_contiguous_dma(reason="1,024 gains, two to a piece, once"):
                    nc.sync.dma_start(out=gain[:], in_=norm_w.rearrange("(a p e) -> p a e", p=P, e=2))
        load_weights(0)
        for m in range(STEP_TILES, SWEEP_TILES):
            load_tokens(m)
        for c in range(1, CHUNKS):
            load_weights(c)
            if c % 2 == 1 and SWEEP_TILES <= c + 1 < TOKEN_TILES:
                load_tokens(c + 1)
                load_tokens(c + 2)

        ident = keep.tile([P, P], F32, name="ident")
        make_identity(nc, ident[:])
        minus_half = keep.tile([P, STEP_TILES], F32, name="minus_half")
        nc.gpsimd.memset(minus_half[:], -0.5)
        warm = keep.tile([P, 1], F32, name="warm")
        nc.scalar.activation(out=warm[:], in_=minus_half[:, 0:1], func=ACT.Gelu)

        x_codes = [keep.tile([P, PASSES * P], U32, name="x_codes%d" % m, align_bytes=64) for m in range(TOKEN_TILES)]
        x_scales = [keep.tile([P, PASSES * P], U8, name="x_scales%d" % m, align_bytes=64) for m in range(TOKEN_TILES)]
        w_codes = [keep.tile([P, PASSES * CHUNK], U32, name="w_codes%d" % c, align_bytes=64) for c in range(CHUNKS)]
        w_scales = [keep.tile([P, PASSES * CHUNK], U8, name="w_scales%d" % c, align_bytes=64) for c in range(CHUNKS)]
        normed = {}
        x_grouped = {}
        w_grouped = {}

        def normalise(tiles):
            count = len(tiles)
            mean_var = small.tile([P, count, 2], F32, name="mean_var")
            for i, m in enumerate(tiles):
                stats = small.tile([P, K // BN_MAX, 6], F32, name="stats")
                for h in range(K // BN_MAX):
                    nc.vector.bn_stats(out=stats[:, h, :], in_=x_in[m][:, BN_MAX * h : BN_MAX * (h + 1)])
                nc.vector.bn_aggr(out=mean_var[:, i, :], in_=stats[:].rearrange("p h s -> p (h s)"))
            neg_mean = small.tile([P, count], F32, name="neg_mean")
            nc.gpsimd.tensor_scalar(
                out=neg_mean[:], in0=mean_var[:, :, 0], scalar1=-1.0, scalar2=0.0, op0=ALU.mult, op1=ALU.add
            )
            var_eps = small.tile([P, count], F32, name="var_eps")
            nc.gpsimd.tensor_scalar(
                out=var_eps[:], in0=mean_var[:, :, 1], scalar1=1.0, scalar2=EPS, op0=ALU.mult, op1=ALU.add
            )
            rstd = small.tile([P, count], F32, name="rstd")
            nc.gpsimd.tensor_tensor(out=rstd[:], in0=var_eps[:], in1=minus_half[:, 0:count], op=ALU.pow)
            for i, m in enumerate(tiles):
                y = work.tile([P, K], F32, name="y")
                nc.gpsimd.tensor_scalar(
                    out=y[:].rearrange("r (a e q) -> r a e q", e=2, q=P),
                    in0=x_in[m][:].rearrange("r (a q e) -> r a e q", e=2, q=P),
                    scalar1=neg_mean[:, i : i + 1],
                    scalar2=rstd[:, i : i + 1],
                    op0=ALU.add,
                    op1=ALU.mult,
                )
                normed[m] = y

        def transpose_tokens(m):
            y = normed[m]
            grouped = work.tile([P, PASSES, P, PACK], BF16, name="x_grouped", bufs=X_GROUPED_BUFS, align_bytes=64)
            for g in range(PASSES):
                yt = banks.tile([P, PACK, P], F32, name="yt", tag="bank")
                for t in range(PACK):
                    block = PACK * g + t
                    nc.tensor.transpose(yt[:, t, :], y[:, P * block : P * (block + 1)], ident[:])
                nc.vector.tensor_tensor(
                    out=grouped[:, g, :, :],
                    in0=yt[:].rearrange("p t r -> p r t"),
                    in1=gain_cols[:, PACK * g : PACK * (g + 1)].unsqueeze(1).to_broadcast([P, P, PACK]),
                    op=ALU.mult,
                )
            x_grouped[m] = grouped

        def quantise_tokens(m):
            nc.vector.quantize_mx(
                out=x_codes[m][:].bitcast(FP8X4),
                scales=x_scales[m][:],
                in_=x_grouped[m][:].rearrange("p g r t -> p (g r t)"),
            )

        def transpose_weights(c):
            words = w_in[c][:].bitcast(F32)
            grouped = work.tile([P, PASSES, CHUNK, PACK], BF16, name="w_grouped", bufs=W_GROUPED_BUFS, align_bytes=64)
            grouped_words = grouped[:].bitcast(F32)
            for i in range(ROW_TILES):
                wt = banks.tile([P, QUARTERS, P], F32, name="wt", tag="bank")
                for a in range(QUARTERS):
                    nc.tensor.transpose(wt[:, a, :], words[:, i, P * a : P * (a + 1)], ident[:])
                nc.scalar.copy(
                    out=grouped_words[:, :, P * i : P * (i + 1), :],
                    in_=wt[:].rearrange("p (g u) n -> p g n u", u=2),
                )
            w_grouped[c] = grouped

        def quantise_weights(c):
            nc.vector.quantize_mx(
                out=w_codes[c][:].bitcast(FP8X4),
                scales=w_scales[c][:],
                in_=w_grouped[c][:].rearrange("p g n t -> p (g n t)"),
            )

        def project(m, c, first=0, width=CHUNK):
            acc = banks.tile([P, width], F32, name="acc", tag="bank")
            for g in range(PASSES):
                features = slice(CHUNK * g + first, CHUNK * g + first + width)
                nc.tensor.matmul_mx(
                    out=acc[:],
                    lhsT=x_codes[m][:, P * g : P * (g + 1)].bitcast(FP8X4),
                    lhsT_scale=x_scales[m][:, P * g : P * (g + 1)],
                    rhs=w_codes[c][:, features].bitcast(FP8X4),
                    rhs_scale=w_scales[c][:, features],
                    start=(g == 0),
                    stop=(g == PASSES - 1),
                )
            return acc

        def gated_step(pair, first_tile, last_pieces=1):
            tiles = range(first_tile, first_tile + STEP_TILES)
            gates = {}
            for m in tiles:
                pre = project(m, 2 * pair)
                gates[m] = results.tile([P, CHUNK], F32, name="gate", bufs=GATE_BUFS)
                nc.scalar.activation(out=gates[m][:], in_=pre[:], func=ACT.Gelu)
            for m in tiles:
                width = CHUNK // (last_pieces if m == tiles[-1] else 1)
                for first in range(0, CHUNK, width):
                    lin = project(m, 2 * pair + 1, first, width)
                    gated = results.tile([P, width], F32, name="gated", tag="out")
                    nc.vector.tensor_tensor(out=gated[:], in0=lin[:], in1=gates[m][:, first : first + width], op=ALU.mult)
                    nc.sync.dma_start(
                        out=geglu_rows[:, m, CHUNK * pair + first : CHUNK * pair + first + width], in_=gated[:]
                    )

        def qk_step(first_tile):
            for m in range(first_tile, first_tile + SWEEP_TILES):
                acc = project(m, QK_CHUNK)
                qk = results.tile([P, CHUNK], F32, name="qk", tag="out")
                if m % 2 == 0:
                    nc.scalar.copy(out=qk[:], in_=acc[:])
                else:
                    nc.vector.tensor_copy(out=qk[:], in_=acc[:])
                nc.sync.dma_start(out=q_rows[:, m, :], in_=qk[:, 0:QK])
                nc.sync.dma_start(out=k_rows[:, m, :], in_=qk[:, QK : 2 * QK])

        steps = []
        for pair in range(PAIRS):
            for half in range(SWEEP_TILES // STEP_TILES):
                steps.append((pair, STEP_TILES * half))
        steps.append((QK_STEP, 0))
        for half in range(SWEEP_TILES // STEP_TILES):
            if half == SWEEP_TILES // STEP_TILES - 1:
                steps.append((QK_STEP, SWEEP_TILES))
            for pair in range(PAIRS):
                steps.append((pair, SWEEP_TILES + STEP_TILES * half))

        def late_tile(s, delay):
            i, rest = divmod(s - delay, LATE_EVERY)
            if rest == 0 and 0 <= i < TOKEN_TILES - SWEEP_TILES:
                return SWEEP_TILES + i
            return None

        for m in range(STEP_TILES):
            normalise([m])
        normalise(list(range(STEP_TILES, SWEEP_TILES)))
        for m in range(SWEEP_TILES):
            transpose_weights(m)
            if 0 < m < SWEEP_TILES - 1:
                quantise_weights(m - 1)
            transpose_tokens(m)
            if m % STEP_TILES == STEP_TILES - 1:
                for ready in range(m - STEP_TILES + 1, m + 1):
                    quantise_tokens(ready)
        quantise_weights(SWEEP_TILES - 2)

        for s, (pair, first_tile) in enumerate(steps):
            if pair == QK_STEP:
                qk_step(first_tile)
            else:
                gated_step(pair, first_tile, last_pieces=(END_PIECES if s == len(steps) - 1 else 1))
            if s + AHEAD < CHUNKS:
                quantise_weights(s + AHEAD)
            if s + AHEAD + 1 < CHUNKS:
                transpose_weights(s + AHEAD + 1)
            if late_tile(s, LATE_QUANTISE) is not None:
                quantise_tokens(late_tile(s, LATE_QUANTISE))
            if late_tile(s, 0) is not None:
                normalise([late_tile(s, 0)])
            if late_tile(s, LATE_TRANSPOSE) is not None:
                transpose_tokens(late_tile(s, LATE_TRANSPOSE))
